import numpy as np
import ml_dtypes


def mxq(x, axis, fmt="e4m3"):
    dtype, down = {"e4m3": (ml_dtypes.float8_e4m3fn, 7), "e5m2": (ml_dtypes.float8_e5m2, 14)}[fmt]
    v = np.moveaxis(np.asarray(x, np.float32).astype(ml_dtypes.bfloat16).astype(np.float64), axis, -1)
    blocks = v.reshape(v.shape[:-1] + (-1, 32))
    amax = np.abs(blocks).max(-1, keepdims=True)
    byte = np.maximum(np.where(amax > 0, np.frexp(amax)[1] - 1 + 127, 0) - down, 1)
    scale = np.exp2(byte - 127.0)
    codes = (blocks / scale).astype(np.float32).astype(dtype).astype(np.float64)
    return np.moveaxis((codes * scale).reshape(v.shape), -1, axis)


WIDE = False


def mx_kscale(k):
    if not WIDE:
        return np.ones(k)
    levels = np.array([10, -10, 5, -5, 0])
    a = np.random.permutation(np.resize(levels, k // 512 * 4)).reshape(k // 512, 4)
    idx = np.arange(k)
    return np.exp2(a[idx // 512, idx % 128 // 32])


BF16 = ml_dtypes.bfloat16


def bf(x):
    return np.asarray(x, np.float32).astype(BF16)


def f64(x):
    return np.asarray(x).astype(np.float64)


B, D_IN, D_HID, D_OUT, LAT = 512, 192, 16384, 512, 16
BN_EPS = 1e-5
L2_EPS = 1e-12


def setup_inputs():
    t = mx_kscale(D_HID)
    col_sd = np.exp(0.4 * np.random.standard_normal(D_HID))
    col_mean = 0.5 * np.random.standard_normal(D_HID)
    return {
        "y_lin": bf(np.random.standard_normal((B, D_HID)) * col_sd + col_mean),
        "gamma": bf((1.0 + 0.2 * np.random.standard_normal(D_HID)) * t),
        "beta": bf(0.3 * np.random.standard_normal(D_HID) * t),
        "W2": bf(np.random.standard_normal((D_OUT, D_HID)) / np.sqrt(D_HID) / t[None, :]),
        "b2": bf(0.2 * np.random.standard_normal(D_OUT)),
    }


def reference(y_lin, gamma, beta, W2, b2):
    y = f64(y_lin)
    mean = np.mean(y, axis=0)
    var = np.mean((y - mean) ** 2, axis=0)
    y = (y - mean) * (1.0 / np.sqrt(var + BN_EPS)) * f64(gamma) + f64(beta)
    a = np.maximum(y, 0.0)
    p = (mxq(a, 1, "e4m3") @ mxq(f64(W2), 1, "e4m3").T) + f64(b2)
    n = np.sqrt(np.sum(p * p, axis=1, keepdims=True))
    return p / np.maximum(n, L2_EPS)

@@ -1,0 +1,267 @@
+from contextlib import ExitStack
+
+import concourse.mybir as mybir
+from concourse.masks import make_identity
+
+F32 = mybir.dt.float32
+BF16 = mybir.dt.bfloat16
+U32 = mybir.dt.uint32
+U8 = mybir.dt.uint8
+FP8X4 = mybir.dt.float8_e4m3fn_x4
+ALU = mybir.AluOpType
+ACT = mybir.ActivationFunctionType
+
+P = 128
+BATCH = 512
+HIDDEN = 16384
+WIDTH = 512
+ROW_TILES = 4
+PACK = 4
+K_PASS = P * PACK
+N_PASS = HIDDEN // K_PASS
+HALVES = 2
+PAIR = 2
+PASS_WORDS = K_PASS // PAIR
+ROUND_PASSES = 2
+ROUND_K = ROUND_PASSES * K_PASS
+N_ROUNDS = N_PASS // ROUND_PASSES
+ROUND_PLANES = ROUND_PASSES * HALVES
+BN_EPS = 1e-5
+L2_EPS = 1e-12
+STATS_MAX = 512
+RUN = 4
+
+STATS_LEAD = 4
+WEIGHT_LEAD = 2
+PACK_LAG = 1
+MATMUL_LAG = 2
+LOAD_AHEAD = 2
+
+FLOPS = 2 * BATCH * WIDTH * HIDDEN
+
+
+def tile_simclr_pa_k_kernel(tc, y_lin, gamma, beta, W2, b2, out):
+    nc = tc.nc
+    with ExitStack() as ctx:
+        ctx.enter_context(tc.manual_schedule())
+        const = ctx.enter_context(tc.tile_pool(name="const", bufs=1))
+        y_pool = ctx.enter_context(tc.tile_pool(name="y_rows", bufs=6))
+        w_pool = ctx.enter_context(tc.tile_pool(name="w_rows", bufs=4))
+        stat_pool = ctx.enter_context(tc.tile_pool(name="statistics", bufs=3))
+        affine_pool = ctx.enter_context(tc.tile_pool(name="affine", bufs=4))
+        stage = ctx.enter_context(tc.tile_pool(name="stage", bufs=3))
+        y_mx = ctx.enter_context(tc.tile_pool(name="y_mx", bufs=3))
+        w_mx = ctx.enter_context(tc.tile_pool(name="w_mx", bufs=6))
+        tail = ctx.enter_context(tc.tile_pool(name="tail", bufs=ROW_TILES))
+        acc_pool = ctx.enter_context(tc.psum_pool(name="acc", bufs=1))
+        vector_banks = ctx.enter_context(tc.psum_pool(name="vector_banks", bufs=2))
+        scalar_banks = ctx.enter_context(tc.psum_pool(name="scalar_banks", bufs=2))
+
+        y_rows = {}
+        w_rows = {}
+        stats = {}
+        scale = {}
+        shift = {}
+        planes = {}
+        y_codes = {}
+        y_scales = {}
+        w_grouped = {}
+        w_codes = {}
+        w_scales = {}
+
+        def load_round(pool, source, r):
+            rows = pool.tile([P, ROW_TILES, ROUND_K], BF16, tag="rows")
+            nc.sync.dma_start(
+                out=rows[:],
+                in_=source.rearrange("(t p) k -> p t k", p=P)[:, :, r * ROUND_K : (r + 1) * ROUND_K],
+            )
+            return rows
+
+        def transpose_words(dest, rows, t, g, u):
+            first = (g % ROUND_PASSES) * PASS_WORDS + u * P
+            nc.tensor.transpose(dest, rows[:].bitcast(F32)[:, t, first : first + P], identity[:])
+
+        def transposed_y(banks, g, u):
+            bank = banks.tile([P, BATCH], F32, tag="bank")
+            for t in range(ROW_TILES):
+                transpose_words(bank[:, t * P : (t + 1) * P], y_rows[g // ROUND_PASSES], t, g, u)
+            return bank
+
+        def read_statistics(g):
+            r = g // ROUND_PASSES
+            if g % ROUND_PASSES == 0:
+                six = stat_pool.tile([P, ROUND_PLANES, 2, 6], F32, tag="six")
+                stats[r] = six
+            for u in range(HALVES):
+                bank = transposed_y(vector_banks, g, u)
+                values = bank[:].bitcast(BF16)
+                for h in range(2):
+                    nc.vector.bn_stats(
+                        out=stats[r][:, (g % ROUND_PASSES) * HALVES + u, h, :],
+                        in_=values[:, h * STATS_MAX : (h + 1) * STATS_MAX],
+                    )
+
+        def finish_statistics(r):
+            shape = [P, ROUND_PLANES, PAIR]
+            first = r * ROUND_PLANES * PAIR
+            gamma_r = gamma_beta[:, first : first + ROUND_PLANES * PAIR].rearrange("p (q e) -> p q e", e=PAIR)
+            beta_r = gamma_beta[:, P + first : P + first + ROUND_PLANES * PAIR].rearrange(
+                "p (q e) -> p q e", e=PAIR
+            )
+            by_parity = stats[r][:].rearrange("p q h (e s) -> p q h e s", s=3)
+            mean_a = by_parity[:, :, 0, :, 1]
+            mean_b = by_parity[:, :, 1, :, 1]
+            dev_a = by_parity[:, :, 0, :, 2]
+            dev_b = by_parity[:, :, 1, :, 2]
+            gap = stat_pool.tile(shape, F32, tag="gap")
+            twice_mean = stat_pool.tile(shape, F32, tag="twice_mean")
+            dev = stat_pool.tile(shape, F32, tag="dev")
+            four_var = stat_pool.tile(shape, F32, tag="four_var")
+            half_rstd = stat_pool.tile(shape, F32, tag="half_rstd")
+            half_scale = stat_pool.tile(shape, F32, tag="half_scale")
+            scale_r = affine_pool.tile(shape, F32, tag="scale")
+            shift_r = affine_pool.tile(shape, F32, tag="shift")
+            nc.gpsimd.tensor_tensor(out=gap[:], in0=mean_a, in1=mean_b, op=ALU.subtract)
+            nc.gpsimd.tensor_tensor(out=twice_mean[:], in0=mean_a, in1=mean_b, op=ALU.add)
+            nc.gpsimd.tensor_tensor(out=dev[:], in0=dev_a, in1=dev_b, op=ALU.add)
+            nc.gpsimd.tensor_tensor(out=gap[:], in0=gap[:], in1=gap[:], op=ALU.mult)
+            nc.gpsimd.tensor_scalar(
+                out=dev[:], in0=dev[:], scalar1=1.0 / 128.0, scalar2=4.0 * BN_EPS, op0=ALU.mult, op1=ALU.add
+            )
+            nc.gpsimd.tensor_tensor(out=four_var[:], in0=dev[:], in1=gap[:], op=ALU.add)
+            nc.gpsimd.tensor_tensor(out=half_rstd[:], in0=four_var[:], in1=minus_half[:], op=ALU.pow)
+            nc.gpsimd.tensor_tensor(out=half_scale[:], in0=half_rstd[:], in1=gamma_r, op=ALU.mult)
+            nc.gpsimd.tensor_scalar(
+                out=scale_r[:], in0=half_scale[:], scalar1=2.0, scalar2=0.0, op0=ALU.mult, op1=ALU.add
+            )
+            nc.gpsimd.tensor_tensor(out=twice_mean[:], in0=twice_mean[:], in1=half_scale[:], op=ALU.mult)
+            nc.gpsimd.tensor_tensor(out=shift_r[:], in0=beta_r, in1=twice_mean[:], op=ALU.subtract)
+            scale[r] = scale_r
+            shift[r] = shift_r
+
+        def normalise(g):
+            r = g // ROUND_PASSES
+            a_planes = stage.tile([P, PACK, BATCH], BF16, tag="a_planes")
+            for u in range(HALVES):
+                q = (g % ROUND_PASSES) * HALVES + u
+                bank = transposed_y(scalar_banks, g, u)
+                values = bank[:].bitcast(BF16).rearrange("p (b e) -> p b e", e=PAIR)
+                for e in range(PAIR):
+                    nc.scalar.activation(
+                        out=a_planes[:, PAIR * u + e, :],
+                        in_=values[:, :, e],
+                        func=ACT.Relu,
+                        scale=scale[r][:, q, e : e + 1],
+                        bias=shift[r][:, q, e : e + 1],
+                    )
+            planes[g] = a_planes
+
+        def copy_weights(g):
+            grouped = stage.tile([P, WIDTH * PACK], BF16, tag="w_grouped", align_bytes=64)
+            words = grouped[:].bitcast(F32).rearrange("p (o u) -> p o u", u=HALVES)
+            rows_in_bank = WIDTH // 2
+            for h in range(2):
+                bank = scalar_banks.tile([P, BATCH], F32, tag="bank")
+                by_half = bank[:].rearrange("p (u o) -> p u o", u=HALVES)
+                for u in range(HALVES):
+                    for j in range(rows_in_bank // P):
+                        transpose_words(
+                            by_half[:, u, j * P : (j + 1) * P], w_rows[g // ROUND_PASSES], 2 * h + j, g, u
+                        )
+                nc.scalar.copy(
+                    out=words[:, h * rows_in_bank : (h + 1) * rows_in_bank, :],
+                    in_=by_half.rearrange("p u o -> p o u"),
+                )
+            w_grouped[g] = grouped
+
+        def quantise(pool, grouped, width, tag):
+            codes = pool.tile([P, width], U32, tag=tag + "_codes", align_bytes=64)
+            scales = pool.tile([P, width], U8, tag=tag + "_scales", align_bytes=64)
+            nc.vector.quantize_mx(out=codes[:].bitcast(FP8X4), scales=scales[:], in_=grouped)
+            return codes, scales
+
+        def multiply(g):
+            for t in range(ROW_TILES):
+                rows = slice(t * P, (t + 1) * P)
+                nc.tensor.matmul_mx(
+                    out=acc[t][:],
+                    lhsT=y_codes[g][:, rows].bitcast(FP8X4),
+                    lhsT_scale=y_scales[g][:, rows],
+                    rhs=w_codes[g][:].bitcast(FP8X4),
+                    rhs_scale=w_scales[g][:],
+                    start=(g == 0),
+                    stop=(g == N_PASS - 1),
+                )
+
+        for r in range(LOAD_AHEAD):
+            y_rows[r] = load_round(y_pool, y_lin, r)
+            w_rows[r] = load_round(w_pool, W2, r)
+        vectors = const.tile([P, PAIR * P], BF16)
+        nc.scalar.dma_start(out=vectors[0 : P // 2, :], in_=gamma.rearrange("(r c) -> r c", c=PAIR * P))
+        nc.scalar.dma_start(out=vectors[P // 2 : P, :], in_=beta.rearrange("(r c) -> r c", c=PAIR * P))
+        identity = const.tile([P, P], F32)
+        make_identity(nc, identity[:])
+        minus_half = const.tile([P, ROUND_PLANES, PAIR], F32)
+        nc.vector.memset(minus_half[:], -0.5)
+        one = const.tile([P, 1], F32)
+        nc.vector.memset(one[:], 1.0)
+        nc.scalar.activation(out=one[:], in_=one[:], func=ACT.Sqrt)
+        bank = vector_banks.tile([P, BATCH], F32, tag="bank")
+        nc.tensor.transpose(bank[:, 0:P], vectors[:].bitcast(F32), identity[:])
+        gamma_beta = const.tile([P, PAIR * P], F32)
+        nc.vector.tensor_copy(out=gamma_beta[:], in_=bank[:].bitcast(BF16)[:, 0 : PAIR * P])
+        acc = [acc_pool.tile([P, WIDTH], F32, name="acc%d" % t) for t in range(ROW_TILES)]
+
+        for i in range(-STATS_LEAD, N_PASS + MATMUL_LAG):
+            g_stats = i + STATS_LEAD
+            g_weight = i + WEIGHT_LEAD
+            if 0 <= g_weight < N_PASS:
+                r = g_weight // ROUND_PASSES + LOAD_AHEAD
+                if g_weight % ROUND_PASSES == 0 and r < N_ROUNDS:
+                    w_rows[r] = load_round(w_pool, W2, r)
+                copy_weights(g_weight)
+            if g_stats < N_PASS:
+                r = g_stats // ROUND_PASSES + LOAD_AHEAD
+                if g_stats % ROUND_PASSES == 0 and r < N_ROUNDS:
+                    y_rows[r] = load_round(y_pool, y_lin, r)
+                read_statistics(g_stats)
+                if g_stats % ROUND_PASSES == ROUND_PASSES - 1:
+                    finish_statistics(g_stats // ROUND_PASSES)
+            if 0 <= i < N_PASS:
+                normalise(i)
+            g = i - PACK_LAG
+            if 0 <= g < N_PASS:
+                a_grouped = stage.tile([P, BATCH, PACK], BF16, tag="a_grouped", align_bytes=64)
+                nc.vector.tensor_copy(
+                    out=a_grouped[:].rearrange("p (c j) t -> p c t j", j=RUN),
+                    in_=planes[g][:].rearrange("p t (c j) -> p c t j", j=RUN),
+                )
+            g_w = g + WEIGHT_LEAD
+            if 0 <= g_w < N_PASS:
+                w_codes[g_w], w_scales[g_w] = quantise(w_mx, w_grouped[g_w][:], WIDTH, "w")
+            if 0 <= g < N_PASS:
+                y_codes[g], y_scales[g] = quantise(
+                    y_mx, a_grouped[:].rearrange("p b t -> p (b t)"), BATCH, "y"
+                )
+            if 0 <= i - MATMUL_LAG:
+                multiply(i - MATMUL_LAG)
+
+        bias_rows = const.tile([P, WIDTH], BF16)
+        nc.sync.dma_start(out=bias_rows[:], in_=b2.partition_broadcast(P))
+        logits = []
+        sum_squares = const.tile([P, ROW_TILES], F32)
+        for t in range(ROW_TILES):
+            p_rows = tail.tile([P, WIDTH], F32, tag="p_rows")
+            nc.vector.tensor_tensor(out=p_rows[:], in0=acc[t][:], in1=bias_rows[:], op=ALU.add)
+            squares = tail.tile([P, WIDTH], F32, tag="squares")
+            nc.scalar.activation(
+                out=squares[:], in_=p_rows[:], func=ACT.Square, accum_out=sum_squares[:, t : t + 1]
+            )
+            logits.append(p_rows)
+        norm = const.tile([P, ROW_TILES], F32)
+        nc.scalar.activation(out=norm[:], in_=sum_squares[:], func=ACT.Sqrt)
+        nc.vector.tensor_scalar_max(out=norm[:], in0=norm[:], scalar1=L2_EPS)
+        nc.vector.reciprocal(out=norm[:], in_=norm[:])
+        for t in range(ROW_TILES):
+            nc.vector.tensor_scalar_mul(out=logits[t][:], in0=logits[t][:], scalar1=norm[:, t : t + 1])
+            nc.sync.dma_start(out=out[t * P : (t + 1) * P, :], in_=logits[t][:])

@@ -30,11 +30,13 @@ BN_EPS = 1e-5
 L2_EPS = 1e-12
 STATS_MAX = 512
 RUN = 4
+VECTOR_ROWS = 256
 
 STATS_LEAD = 4
-WEIGHT_LEAD = 2
-PACK_LAG = 1
-MATMUL_LAG = 2
+WEIGHT_LEAD = 4
+GROUP_LAG = 1
+QUANTISE_LAG = 2
+MATMUL_LAG = 4
 LOAD_AHEAD = 2
 
 FLOPS = 2 * BATCH * WIDTH * HIDDEN
@@ -50,8 +52,8 @@ def tile_simclr_pa_k_kernel(tc, y_lin, gamma, beta, W2, b2, out):
         stat_pool = ctx.enter_context(tc.tile_pool(name="statistics", bufs=3))
         affine_pool = ctx.enter_context(tc.tile_pool(name="affine", bufs=4))
         stage = ctx.enter_context(tc.tile_pool(name="stage", bufs=3))
-        y_mx = ctx.enter_context(tc.tile_pool(name="y_mx", bufs=3))
-        w_mx = ctx.enter_context(tc.tile_pool(name="w_mx", bufs=6))
+        y_mx = ctx.enter_context(tc.tile_pool(name="y_mx", bufs=4))
+        w_mx = ctx.enter_context(tc.tile_pool(name="w_mx", bufs=9))
         tail = ctx.enter_context(tc.tile_pool(name="tail", bufs=ROW_TILES))
         acc_pool = ctx.enter_context(tc.psum_pool(name="acc", bufs=1))
         vector_banks = ctx.enter_context(tc.psum_pool(name="vector_banks", bufs=2))
@@ -60,14 +62,20 @@ def tile_simclr_pa_k_kernel(tc, y_lin, gamma, beta, W2, b2, out):
         y_rows = {}
         w_rows = {}
         stats = {}
+        twice_mean = {}
+        four_var = {}
+        twice_std = {}
+        half_rstd = {}
         scale = {}
         shift = {}
-        planes = {}
+        a_planes = {}
+        a_grouped = {}
+        w_grouped = {}
         y_codes = {}
         y_scales = {}
-        w_grouped = {}
         w_codes = {}
         w_scales = {}
+        per_k = [P, ROUND_PLANES, PAIR]
 
         def load_round(pool, source, r):
             rows = pool.tile([P, ROW_TILES, ROUND_K], BF16, tag="rows")
@@ -87,92 +95,99 @@ def tile_simclr_pa_k_kernel(tc, y_lin, gamma, beta, W2, b2, out):
                 transpose_words(bank[:, t * P : (t + 1) * P], y_rows[g // ROUND_PASSES], t, g, u)
             return bank
 
-        def read_statistics(g):
+        def read_statistics(g, u):
             r = g // ROUND_PASSES
-            if g % ROUND_PASSES == 0:
+            if g % ROUND_PASSES == 0 and u == 0:
                 six = stat_pool.tile([P, ROUND_PLANES, 2, 6], F32, tag="six")
                 stats[r] = six
-            for u in range(HALVES):
-                bank = transposed_y(vector_banks, g, u)
-                values = bank[:].bitcast(BF16)
-                for h in range(2):
-                    nc.vector.bn_stats(
-                        out=stats[r][:, (g % ROUND_PASSES) * HALVES + u, h, :],
-                        in_=values[:, h * STATS_MAX : (h + 1) * STATS_MAX],
-                    )
+            bank = transposed_y(vector_banks, g, u)
+            values = bank[:].bitcast(BF16)
+            for h in range(2):
+                nc.vector.bn_stats(
+                    out=stats[r][:, (g % ROUND_PASSES) * HALVES + u, h, :],
+                    in_=values[:, h * STATS_MAX : (h + 1) * STATS_MAX],
+                )
 
-        def finish_statistics(r):
-            shape = [P, ROUND_PLANES, PAIR]
-            first = r * ROUND_PLANES * PAIR
-            gamma_r = gamma_beta[:, first : first + ROUND_PLANES * PAIR].rearrange("p (q e) -> p q e", e=PAIR)
-            beta_r = gamma_beta[:, P + first : P + first + ROUND_PLANES * PAIR].rearrange(
-                "p (q e) -> p q e", e=PAIR
-            )
+        def merge_statistics(r):
             by_parity = stats[r][:].rearrange("p q h (e s) -> p q h e s", s=3)
             mean_a = by_parity[:, :, 0, :, 1]
             mean_b = by_parity[:, :, 1, :, 1]
             dev_a = by_parity[:, :, 0, :, 2]
             dev_b = by_parity[:, :, 1, :, 2]
-            gap = stat_pool.tile(shape, F32, tag="gap")
-            twice_mean = stat_pool.tile(shape, F32, tag="twice_mean")
-            dev = stat_pool.tile(shape, F32, tag="dev")
-            four_var = stat_pool.tile(shape, F32, tag="four_var")
-            half_rstd = stat_pool.tile(shape, F32, tag="half_rstd")
-            half_scale = stat_pool.tile(shape, F32, tag="half_scale")
-            scale_r = affine_pool.tile(shape, F32, tag="scale")
-            shift_r = affine_pool.tile(shape, F32, tag="shift")
+            gap = stat_pool.tile(per_k, F32, tag="gap")
+            dev = stat_pool.tile(per_k, F32, tag="dev")
+            mean2 = stat_pool.tile(per_k, F32, tag="mean2")
+            var4 = stat_pool.tile(per_k, F32, tag="var4")
             nc.gpsimd.tensor_tensor(out=gap[:], in0=mean_a, in1=mean_b, op=ALU.subtract)
-            nc.gpsimd.tensor_tensor(out=twice_mean[:], in0=mean_a, in1=mean_b, op=ALU.add)
             nc.gpsimd.tensor_tensor(out=dev[:], in0=dev_a, in1=dev_b, op=ALU.add)
             nc.gpsimd.tensor_tensor(out=gap[:], in0=gap[:], in1=gap[:], op=ALU.mult)
             nc.gpsimd.tensor_scalar(
                 out=dev[:], in0=dev[:], scalar1=1.0 / 128.0, scalar2=4.0 * BN_EPS, op0=ALU.mult, op1=ALU.add
             )
-            nc.gpsimd.tensor_tensor(out=four_var[:], in0=dev[:], in1=gap[:], op=ALU.add)
-            nc.gpsimd.tensor_tensor(out=half_rstd[:], in0=four_var[:], in1=minus_half[:], op=ALU.pow)
-            nc.gpsimd.tensor_tensor(out=half_scale[:], in0=half_rstd[:], in1=gamma_r, op=ALU.mult)
+            nc.gpsimd.tensor_tensor(out=var4[:], in0=dev[:], in1=gap[:], op=ALU.add)
+            nc.gpsimd.tensor_tensor(out=mean2[:], in0=mean_a, in1=mean_b, op=ALU.add)
+            twice_mean[r] = mean2
+            four_var[r] = var4
+
+        def root_of_variance(r):
+            std2 = stat_pool.tile(per_k, F32, tag="std2")
+            nc.scalar.activation(out=std2[:], in_=four_var[r][:], func=ACT.Sqrt)
+            twice_std[r] = std2
+
+        def invert_deviation(r):
+            rstd = stat_pool.tile(per_k, F32, tag="rstd")
+            nc.vector.reciprocal(out=rstd[:], in_=twice_std[r][:])
+            half_rstd[r] = rstd
+
+        def scale_and_shift(r):
+            first = r * ROUND_PLANES * PAIR
+            count = ROUND_PLANES * PAIR
+            gamma_r = gamma_beta[:, first : first + count].rearrange("p (q e) -> p q e", e=PAIR)
+            beta_r = gamma_beta[:, P + first : P + first + count].rearrange("p (q e) -> p q e", e=PAIR)
+            half_scale = stat_pool.tile(per_k, F32, tag="half_scale")
+            scale_r = affine_pool.tile(per_k, F32, tag="scale")
+            shift_r = affine_pool.tile(per_k, F32, tag="shift")
+            nc.gpsimd.tensor_tensor(out=half_scale[:], in0=half_rstd[r][:], in1=gamma_r, op=ALU.mult)
             nc.gpsimd.tensor_scalar(
                 out=scale_r[:], in0=half_scale[:], scalar1=2.0, scalar2=0.0, op0=ALU.mult, op1=ALU.add
             )
-            nc.gpsimd.tensor_tensor(out=twice_mean[:], in0=twice_mean[:], in1=half_scale[:], op=ALU.mult)
-            nc.gpsimd.tensor_tensor(out=shift_r[:], in0=beta_r, in1=twice_mean[:], op=ALU.subtract)
+            nc.gpsimd.tensor_tensor(out=half_scale[:], in0=half_scale[:], in1=twice_mean[r][:], op=ALU.mult)
+            nc.gpsimd.tensor_tensor(out=shift_r[:], in0=beta_r, in1=half_scale[:], op=ALU.subtract)
             scale[r] = scale_r
             shift[r] = shift_r
 
-        def normalise(g):
+        def normalise(g, u):
             r = g // ROUND_PASSES
-            a_planes = stage.tile([P, PACK, BATCH], BF16, tag="a_planes")
-            for u in range(HALVES):
-                q = (g % ROUND_PASSES) * HALVES + u
-                bank = transposed_y(scalar_banks, g, u)
-                values = bank[:].bitcast(BF16).rearrange("p (b e) -> p b e", e=PAIR)
-                for e in range(PAIR):
-                    nc.scalar.activation(
-                        out=a_planes[:, PAIR * u + e, :],
-                        in_=values[:, :, e],
-                        func=ACT.Relu,
-                        scale=scale[r][:, q, e : e + 1],
-                        bias=shift[r][:, q, e : e + 1],
-                    )
-            planes[g] = a_planes
-
-        def copy_weights(g):
-            grouped = stage.tile([P, WIDTH * PACK], BF16, tag="w_grouped", align_bytes=64)
-            words = grouped[:].bitcast(F32).rearrange("p (o u) -> p o u", u=HALVES)
-            rows_in_bank = WIDTH // 2
-            for h in range(2):
-                bank = scalar_banks.tile([P, BATCH], F32, tag="bank")
-                by_half = bank[:].rearrange("p (u o) -> p u o", u=HALVES)
-                for u in range(HALVES):
-                    for j in range(rows_in_bank // P):
-                        transpose_words(
-                            by_half[:, u, j * P : (j + 1) * P], w_rows[g // ROUND_PASSES], 2 * h + j, g, u
-                        )
-                nc.scalar.copy(
-                    out=words[:, h * rows_in_bank : (h + 1) * rows_in_bank, :],
-                    in_=by_half.rearrange("p u o -> p o u"),
+            q = (g % ROUND_PASSES) * HALVES + u
+            if u == 0:
+                planes = stage.tile([P, PACK, BATCH], BF16, tag="a_planes")
+                a_planes[g] = planes
+            bank = transposed_y(scalar_banks, g, u)
+            values = bank[:].bitcast(BF16).rearrange("p (b e) -> p b e", e=PAIR)
+            for e in range(PAIR):
+                nc.scalar.activation(
+                    out=a_planes[g][:, PAIR * u + e, :],
+                    in_=values[:, :, e],
+                    func=ACT.Relu,
+                    scale=scale[r][:, q, e : e + 1],
+                    bias=shift[r][:, q, e : e + 1],
                 )
-            w_grouped[g] = grouped
+
+        def copy_weights(g, h):
+            if h == 0:
+                grouped = stage.tile([P, WIDTH * PACK], BF16, tag="w_grouped", align_bytes=64)
+                w_grouped[g] = grouped
+            words = w_grouped[g][:].bitcast(F32).rearrange("p (o u) -> p o u", u=HALVES)
+            rows_in_bank = WIDTH // 2
+            bank = scalar_banks.tile([P, BATCH], F32, tag="bank")
+            by_half = bank[:].rearrange("p (u o) -> p u o", u=HALVES)
+            for u in range(HALVES):
+                for j in range(rows_in_bank // P):
+                    transpose_words(by_half[:, u, j * P : (j + 1) * P], w_rows[g // ROUND_PASSES], 2 * h + j, g, u)
+            nc.scalar.copy(
+                out=words[:, h * rows_in_bank : (h + 1) * rows_in_bank, :],
+                in_=by_half.rearrange("p u o -> p o u"),
+            )
 
         def quantise(pool, grouped, width, tag):
             codes = pool.tile([P, width], U32, tag=tag + "_codes", align_bytes=64)
@@ -180,18 +195,23 @@ def tile_simclr_pa_k_kernel(tc, y_lin, gamma, beta, W2, b2, out):
             nc.vector.quantize_mx(out=codes[:].bitcast(FP8X4), scales=scales[:], in_=grouped)
             return codes, scales
 
-        def multiply(g):
-            for t in range(ROW_TILES):
-                rows = slice(t * P, (t + 1) * P)
-                nc.tensor.matmul_mx(
-                    out=acc[t][:],
-                    lhsT=y_codes[g][:, rows].bitcast(FP8X4),
-                    lhsT_scale=y_scales[g][:, rows],
-                    rhs=w_codes[g][:].bitcast(FP8X4),
-                    rhs_scale=w_scales[g][:],
-                    start=(g == 0),
-                    stop=(g == N_PASS - 1),
-                )
+        def multiply(g, t):
+            rows = slice(t * P, (t + 1) * P)
+            nc.tensor.matmul_mx(
+                out=acc[t][:],
+                lhsT=y_codes[g][:, rows].bitcast(FP8X4),
+                lhsT_scale=y_scales[g][:, rows],
+                rhs=w_codes[g][:].bitcast(FP8X4),
+                rhs_scale=w_scales[g][:],
+                start=(g == 0),
+                stop=(g == N_PASS - 1),
+            )
+
+        def in_range(g):
+            return 0 <= g < N_PASS
+
+        def closes_round(g):
+            return in_range(g) and g % ROUND_PASSES == ROUND_PASSES - 1
 
         for r in range(LOAD_AHEAD):
             y_rows[r] = load_round(y_pool, y_lin, r)
@@ -201,8 +221,6 @@ def tile_simclr_pa_k_kernel(tc, y_lin, gamma, beta, W2, b2, out):
         nc.scalar.dma_start(out=vectors[P // 2 : P, :], in_=beta.rearrange("(r c) -> r c", c=PAIR * P))
         identity = const.tile([P, P], F32)
         make_identity(nc, identity[:])
-        minus_half = const.tile([P, ROUND_PLANES, PAIR], F32)
-        nc.vector.memset(minus_half[:], -0.5)
         one = const.tile([P, 1], F32)
         nc.vector.memset(one[:], 1.0)
         nc.scalar.activation(out=one[:], in_=one[:], func=ACT.Sqrt)
@@ -215,41 +233,65 @@ def tile_simclr_pa_k_kernel(tc, y_lin, gamma, beta, W2, b2, out):
         for i in range(-STATS_LEAD, N_PASS + MATMUL_LAG):
             g_stats = i + STATS_LEAD
             g_weight = i + WEIGHT_LEAD
-            if 0 <= g_weight < N_PASS:
-                r = g_weight // ROUND_PASSES + LOAD_AHEAD
-                if g_weight % ROUND_PASSES == 0 and r < N_ROUNDS:
-                    w_rows[r] = load_round(w_pool, W2, r)
-                copy_weights(g_weight)
-            if g_stats < N_PASS:
-                r = g_stats // ROUND_PASSES + LOAD_AHEAD
-                if g_stats % ROUND_PASSES == 0 and r < N_ROUNDS:
-                    y_rows[r] = load_round(y_pool, y_lin, r)
-                read_statistics(g_stats)
-                if g_stats % ROUND_PASSES == ROUND_PASSES - 1:
-                    finish_statistics(g_stats // ROUND_PASSES)
-            if 0 <= i < N_PASS:
-                normalise(i)
-            g = i - PACK_LAG
-            if 0 <= g < N_PASS:
-                a_grouped = stage.tile([P, BATCH, PACK], BF16, tag="a_grouped", align_bytes=64)
+            g_group = i - GROUP_LAG
+            g_quantise = i - QUANTISE_LAG
+            g_multiply = i - MATMUL_LAG
+            for g, rows, pool, source in ((g_stats, y_rows, y_pool, y_lin), (g_weight, w_rows, w_pool, W2)):
+                r = g // ROUND_PASSES + LOAD_AHEAD
+                if g % ROUND_PASSES == 0 and r < N_ROUNDS:
+                    rows[r] = load_round(pool, source, r)
+
+            if in_range(g_group):
+                grouped = stage.tile([P, BATCH, PACK], BF16, tag="a_grouped", align_bytes=64)
+                a_grouped[g_group] = grouped
+                nc.gpsimd.tensor_scalar(
+                    out=grouped[:, VECTOR_ROWS:BATCH, :],
+                    in0=a_planes[g_group][:, :, VECTOR_ROWS:BATCH].rearrange("p t b -> p b t"),
+                    scalar1=1.0,
+                    scalar2=0.0,
+                    op0=ALU.mult,
+                    op1=ALU.add,
+                )
+            if closes_round(g_stats - 2):
+                invert_deviation((g_stats - 2) // ROUND_PASSES)
+                scale_and_shift((g_stats - 2) // ROUND_PASSES)
+
+            for u in range(HALVES):
+                if in_range(g_stats):
+                    read_statistics(g_stats, u)
+                if in_range(g_weight):
+                    copy_weights(g_weight, u)
+                if in_range(i):
+                    normalise(i, u)
+                if in_range(g_multiply):
+                    multiply(g_multiply, 2 * u)
+                    multiply(g_multiply, 2 * u + 1)
+
+            if closes_round(g_stats):
+                merge_statistics(g_stats // ROUND_PASSES)
+            if closes_round(g_stats - 1):
+                root_of_variance((g_stats - 1) // ROUND_PASSES)
+
+            if in_range(g_group):
                 nc.vector.tensor_copy(
-                    out=a_grouped[:].rearrange("p (c j) t -> p c t j", j=RUN),
-                    in_=planes[g][:].rearrange("p t (c j) -> p c t j", j=RUN),
+                    out=a_grouped[g_group][:, 0:VECTOR_ROWS, :].rearrange("p (c j) t -> p c t j", j=RUN),
+                    in_=a_planes[g_group][:, :, 0:VECTOR_ROWS].rearrange("p t (c j) -> p c t j", j=RUN),
                 )
-            g_w = g + WEIGHT_LEAD
-            if 0 <= g_w < N_PASS:
-                w_codes[g_w], w_scales[g_w] = quantise(w_mx, w_grouped[g_w][:], WIDTH, "w")
-            if 0 <= g < N_PASS:
-                y_codes[g], y_scales[g] = quantise(
-                    y_mx, a_grouped[:].rearrange("p b t -> p (b t)"), BATCH, "y"
+            if in_range(g_weight - 1):
+                w_codes[g_weight - 1], w_scales[g_weight - 1] = quantise(
+                    w_mx, w_grouped[g_weight - 1][:], WIDTH, "w"
                 )
-            if 0 <= i - MATMUL_LAG:
-                multiply(i - MATMUL_LAG)
+            if in_range(g_quantise):
+                y_codes[g_quantise], y_scales[g_quantise] = quantise(
+                    y_mx, a_grouped[g_quantise][:].rearrange("p b t -> p (b t)"), BATCH, "y"
+                )
 
         bias_rows = const.tile([P, WIDTH], BF16)
         nc.sync.dma_start(out=bias_rows[:], in_=b2.partition_broadcast(P))
         logits = []
         sum_squares = const.tile([P, ROW_TILES], F32)
+        norm = const.tile([P, ROW_TILES], F32)
+        factor = const.tile([P, ROW_TILES], F32)
         for t in range(ROW_TILES):
             p_rows = tail.tile([P, WIDTH], F32, tag="p_rows")
             nc.vector.tensor_tensor(out=p_rows[:], in0=acc[t][:], in1=bias_rows[:], op=ALU.add)
@@ -257,11 +299,10 @@ def tile_simclr_pa_k_kernel(tc, y_lin, gamma, beta, W2, b2, out):
             nc.scalar.activation(
                 out=squares[:], in_=p_rows[:], func=ACT.Square, accum_out=sum_squares[:, t : t + 1]
             )
+            nc.scalar.activation(out=norm[:, t : t + 1], in_=sum_squares[:, t : t + 1], func=ACT.Sqrt)
             logits.append(p_rows)
-        norm = const.tile([P, ROW_TILES], F32)
-        nc.scalar.activation(out=norm[:], in_=sum_squares[:], func=ACT.Sqrt)
-        nc.vector.tensor_scalar_max(out=norm[:], in0=norm[:], scalar1=L2_EPS)
-        nc.vector.reciprocal(out=norm[:], in_=norm[:])
         for t in range(ROW_TILES):
-            nc.vector.tensor_scalar_mul(out=logits[t][:], in0=logits[t][:], scalar1=norm[:, t : t + 1])
+            nc.vector.tensor_scalar_max(out=factor[:, t : t + 1], in0=norm[:, t : t + 1], scalar1=L2_EPS)
+            nc.vector.reciprocal(out=factor[:, t : t + 1], in_=factor[:, t : t + 1])
+            nc.vector.tensor_scalar_mul(out=logits[t][:], in0=logits[t][:], scalar1=factor[:, t : t + 1])
             nc.sync.dma_start(out=out[t * P : (t + 1) * P, :], in_=logits[t][:])

@@ -32,11 +32,10 @@ STATS_MAX = 512
 RUN = 4
 VECTOR_ROWS = 256
 
-STATS_LEAD = 4
+STATS_LEAD = 5
 WEIGHT_LEAD = 4
 GROUP_LAG = 1
-QUANTISE_LAG = 2
-MATMUL_LAG = 4
+MATMUL_LAG = 3
 LOAD_AHEAD = 2
 
 FLOPS = 2 * BATCH * WIDTH * HIDDEN
@@ -54,6 +53,7 @@ def tile_simclr_pa_k_kernel(tc, y_lin, gamma, beta, W2, b2, out):
         stage = ctx.enter_context(tc.tile_pool(name="stage", bufs=3))
         y_mx = ctx.enter_context(tc.tile_pool(name="y_mx", bufs=4))
         w_mx = ctx.enter_context(tc.tile_pool(name="w_mx", bufs=9))
+        shared = ctx.enter_context(tc.tile_pool(name="shared", bufs=1))
         tail = ctx.enter_context(tc.tile_pool(name="tail", bufs=ROW_TILES))
         acc_pool = ctx.enter_context(tc.psum_pool(name="acc", bufs=1))
         vector_banks = ctx.enter_context(tc.psum_pool(name="vector_banks", bufs=2))
@@ -234,15 +234,14 @@ def tile_simclr_pa_k_kernel(tc, y_lin, gamma, beta, W2, b2, out):
             g_stats = i + STATS_LEAD
             g_weight = i + WEIGHT_LEAD
             g_group = i - GROUP_LAG
-            g_quantise = i - QUANTISE_LAG
             g_multiply = i - MATMUL_LAG
             for g, rows, pool, source in ((g_stats, y_rows, y_pool, y_lin), (g_weight, w_rows, w_pool, W2)):
                 r = g // ROUND_PASSES + LOAD_AHEAD
-                if g % ROUND_PASSES == 0 and r < N_ROUNDS:
+                if in_range(g) and g % ROUND_PASSES == 0 and r < N_ROUNDS:
                     rows[r] = load_round(pool, source, r)
 
             if in_range(g_group):
-                grouped = stage.tile([P, BATCH, PACK], BF16, tag="a_grouped", align_bytes=64)
+                grouped = shared.tile([P, BATCH, PACK], BF16, tag="a_grouped", align_bytes=64)
                 a_grouped[g_group] = grouped
                 nc.gpsimd.tensor_scalar(
                     out=grouped[:, VECTOR_ROWS:BATCH, :],
@@ -252,20 +251,21 @@ def tile_simclr_pa_k_kernel(tc, y_lin, gamma, beta, W2, b2, out):
                     op0=ALU.mult,
                     op1=ALU.add,
                 )
-            if closes_round(g_stats - 2):
-                invert_deviation((g_stats - 2) // ROUND_PASSES)
-                scale_and_shift((g_stats - 2) // ROUND_PASSES)
+            if closes_round(g_stats - 3):
+                invert_deviation((g_stats - 3) // ROUND_PASSES)
+                scale_and_shift((g_stats - 3) // ROUND_PASSES)
 
             for u in range(HALVES):
-                if in_range(g_stats):
-                    read_statistics(g_stats, u)
                 if in_range(g_weight):
                     copy_weights(g_weight, u)
-                if in_range(i):
+                if in_range(g_stats):
+                    read_statistics(g_stats, u)
+            if in_range(i):
+                for u in range(HALVES):
                     normalise(i, u)
-                if in_range(g_multiply):
-                    multiply(g_multiply, 2 * u)
-                    multiply(g_multiply, 2 * u + 1)
+            if in_range(g_multiply):
+                for t in range(ROW_TILES):
+                    multiply(g_multiply, t)
 
             if closes_round(g_stats):
                 merge_statistics(g_stats // ROUND_PASSES)
@@ -281,9 +281,9 @@ def tile_simclr_pa_k_kernel(tc, y_lin, gamma, beta, W2, b2, out):
                 w_codes[g_weight - 1], w_scales[g_weight - 1] = quantise(
                     w_mx, w_grouped[g_weight - 1][:], WIDTH, "w"
                 )
-            if in_range(g_quantise):
-                y_codes[g_quantise], y_scales[g_quantise] = quantise(
-                    y_mx, a_grouped[g_quantise][:].rearrange("p b t -> p (b t)"), BATCH, "y"
+            if in_range(g_group):
+                y_codes[g_group], y_scales[g_group] = quantise(
+                    y_mx, a_grouped[g_group][:].rearrange("p b t -> p (b t)"), BATCH, "y"
                 )
 
         bias_rows = const.tile([P, WIDTH], BF16)

from contextlib import ExitStack

import concourse.mybir as mybir
from concourse.masks import make_identity

F32 = mybir.dt.float32
BF16 = mybir.dt.bfloat16
U32 = mybir.dt.uint32
U8 = mybir.dt.uint8
FP8X4 = mybir.dt.float8_e4m3fn_x4
ALU = mybir.AluOpType
ACT = mybir.ActivationFunctionType

P = 128
BATCH = 512
HIDDEN = 16384
WIDTH = 512
ROW_TILES = 4
PACK = 4
K_PASS = P * PACK
N_PASS = HIDDEN // K_PASS
HALVES = 2
PAIR = 2
PASS_WORDS = K_PASS // PAIR
ROUND_PASSES = 2
ROUND_K = ROUND_PASSES * K_PASS
N_ROUNDS = N_PASS // ROUND_PASSES
ROUND_PLANES = ROUND_PASSES * HALVES
BN_EPS = 1e-5
L2_EPS = 1e-12
STATS_MAX = 512
RUN = 4
VECTOR_ROWS = 256

STATS_LEAD = 5
WEIGHT_LEAD = 4
GROUP_LAG = 1
MATMUL_LAG = 3
LOAD_AHEAD = 2

FLOPS = 2 * BATCH * WIDTH * HIDDEN


def tile_simclr_pa_k_kernel(tc, y_lin, gamma, beta, W2, b2, out):
    nc = tc.nc
    with ExitStack() as ctx:
        ctx.enter_context(tc.manual_schedule())
        const = ctx.enter_context(tc.tile_pool(name="const", bufs=1))
        y_pool = ctx.enter_context(tc.tile_pool(name="y_rows", bufs=6))
        w_pool = ctx.enter_context(tc.tile_pool(name="w_rows", bufs=4))
        stat_pool = ctx.enter_context(tc.tile_pool(name="statistics", bufs=3))
        affine_pool = ctx.enter_context(tc.tile_pool(name="affine", bufs=4))
        stage = ctx.enter_context(tc.tile_pool(name="stage", bufs=3))
        y_mx = ctx.enter_context(tc.tile_pool(name="y_mx", bufs=4))
        w_mx = ctx.enter_context(tc.tile_pool(name="w_mx", bufs=9))
        shared = ctx.enter_context(tc.tile_pool(name="shared", bufs=1))
        tail = ctx.enter_context(tc.tile_pool(name="tail", bufs=ROW_TILES))
        acc_pool = ctx.enter_context(tc.psum_pool(name="acc", bufs=1))
        vector_banks = ctx.enter_context(tc.psum_pool(name="vector_banks", bufs=2))
        scalar_banks = ctx.enter_context(tc.psum_pool(name="scalar_banks", bufs=2))

        y_rows = {}
        w_rows = {}
        stats = {}
        twice_mean = {}
        four_var = {}
        twice_std = {}
        half_rstd = {}
        scale = {}
        shift = {}
        a_planes = {}
        a_grouped = {}
        w_grouped = {}
        y_codes = {}
        y_scales = {}
        w_codes = {}
        w_scales = {}
        per_k = [P, ROUND_PLANES, PAIR]

        def load_round(pool, source, r):
            rows = pool.tile([P, ROW_TILES, ROUND_K], BF16, tag="rows")
            nc.sync.dma_start(
                out=rows[:],
                in_=source.rearrange("(t p) k -> p t k", p=P)[:, :, r * ROUND_K : (r + 1) * ROUND_K],
            )
            return rows

        def transpose_words(dest, rows, t, g, u):
            first = (g % ROUND_PASSES) * PASS_WORDS + u * P
            nc.tensor.transpose(dest, rows[:].bitcast(F32)[:, t, first : first + P], identity[:])

        def transposed_y(banks, g, u):
            bank = banks.tile([P, BATCH], F32, tag="bank")
            for t in range(ROW_TILES):
                transpose_words(bank[:, t * P : (t + 1) * P], y_rows[g // ROUND_PASSES], t, g, u)
            return bank

        def read_statistics(g, u):
            r = g // ROUND_PASSES
            if g % ROUND_PASSES == 0 and u == 0:
                six = stat_pool.tile([P, ROUND_PLANES, 2, 6], F32, tag="six")
                stats[r] = six
            bank = transposed_y(vector_banks, g, u)
            values = bank[:].bitcast(BF16)
            for h in range(2):
                nc.vector.bn_stats(
                    out=stats[r][:, (g % ROUND_PASSES) * HALVES + u, h, :],
                    in_=values[:, h * STATS_MAX : (h + 1) * STATS_MAX],
                )

        def merge_statistics(r):
            by_parity = stats[r][:].rearrange("p q h (e s) -> p q h e s", s=3)
            mean_a = by_parity[:, :, 0, :, 1]
            mean_b = by_parity[:, :, 1, :, 1]
            dev_a = by_parity[:, :, 0, :, 2]
            dev_b = by_parity[:, :, 1, :, 2]
            gap = stat_pool.tile(per_k, F32, tag="gap")
            dev = stat_pool.tile(per_k, F32, tag="dev")
            mean2 = stat_pool.tile(per_k, F32, tag="mean2")
            var4 = stat_pool.tile(per_k, F32, tag="var4")
            nc.gpsimd.tensor_tensor(out=gap[:], in0=mean_a, in1=mean_b, op=ALU.subtract)
            nc.gpsimd.tensor_tensor(out=dev[:], in0=dev_a, in1=dev_b, op=ALU.add)
            nc.gpsimd.tensor_tensor(out=gap[:], in0=gap[:], in1=gap[:], op=ALU.mult)
            nc.gpsimd.tensor_scalar(
                out=dev[:], in0=dev[:], scalar1=1.0 / 128.0, scalar2=4.0 * BN_EPS, op0=ALU.mult, op1=ALU.add
            )
            nc.gpsimd.tensor_tensor(out=var4[:], in0=dev[:], in1=gap[:], op=ALU.add)
            nc.gpsimd.tensor_tensor(out=mean2[:], in0=mean_a, in1=mean_b, op=ALU.add)
            twice_mean[r] = mean2
            four_var[r] = var4

        def root_of_variance(r):
            std2 = stat_pool.tile(per_k, F32, tag="std2")
            nc.scalar.activation(out=std2[:], in_=four_var[r][:], func=ACT.Sqrt)
            twice_std[r] = std2

        def invert_deviation(r):
            rstd = stat_pool.tile(per_k, F32, tag="rstd")
            nc.vector.reciprocal(out=rstd[:], in_=twice_std[r][:])
            half_rstd[r] = rstd

        def scale_and_shift(r):
            first = r * ROUND_PLANES * PAIR
            count = ROUND_PLANES * PAIR
            gamma_r = gamma_beta[:, first : first + count].rearrange("p (q e) -> p q e", e=PAIR)
            beta_r = gamma_beta[:, P + first : P + first + count].rearrange("p (q e) -> p q e", e=PAIR)
            half_scale = stat_pool.tile(per_k, F32, tag="half_scale")
            scale_r = affine_pool.tile(per_k, F32, tag="scale")
            shift_r = affine_pool.tile(per_k, F32, tag="shift")
            nc.gpsimd.tensor_tensor(out=half_scale[:], in0=half_rstd[r][:], in1=gamma_r, op=ALU.mult)
            nc.gpsimd.tensor_scalar(
                out=scale_r[:], in0=half_scale[:], scalar1=2.0, scalar2=0.0, op0=ALU.mult, op1=ALU.add
            )
            nc.gpsimd.tensor_tensor(out=half_scale[:], in0=half_scale[:], in1=twice_mean[r][:], op=ALU.mult)
            nc.gpsimd.tensor_tensor(out=shift_r[:], in0=beta_r, in1=half_scale[:], op=ALU.subtract)
            scale[r] = scale_r
            shift[r] = shift_r

        def normalise(g, u):
            r = g // ROUND_PASSES
            q = (g % ROUND_PASSES) * HALVES + u
            if u == 0:
                planes = stage.tile([P, PACK, BATCH], BF16, tag="a_planes")
                a_planes[g] = planes
            bank = transposed_y(scalar_banks, g, u)
            values = bank[:].bitcast(BF16).rearrange("p (b e) -> p b e", e=PAIR)
            for e in range(PAIR):
                nc.scalar.activation(
                    out=a_planes[g][:, PAIR * u + e, :],
                    in_=values[:, :, e],
                    func=ACT.Relu,
                    scale=scale[r][:, q, e : e + 1],
                    bias=shift[r][:, q, e : e + 1],
                )

        def copy_weights(g, h):
            if h == 0:
                grouped = stage.tile([P, WIDTH * PACK], BF16, tag="w_grouped", align_bytes=64)
                w_grouped[g] = grouped
            words = w_grouped[g][:].bitcast(F32).rearrange("p (o u) -> p o u", u=HALVES)
            rows_in_bank = WIDTH // 2
            bank = scalar_banks.tile([P, BATCH], F32, tag="bank")
            by_half = bank[:].rearrange("p (u o) -> p u o", u=HALVES)
            for u in range(HALVES):
                for j in range(rows_in_bank // P):
                    transpose_words(by_half[:, u, j * P : (j + 1) * P], w_rows[g // ROUND_PASSES], 2 * h + j, g, u)
            nc.scalar.copy(
                out=words[:, h * rows_in_bank : (h + 1) * rows_in_bank, :],
                in_=by_half.rearrange("p u o -> p o u"),
            )

        def quantise(pool, grouped, width, tag):
            codes = pool.tile([P, width], U32, tag=tag + "_codes", align_bytes=64)
            scales = pool.tile([P, width], U8, tag=tag + "_scales", align_bytes=64)
            nc.vector.quantize_mx(out=codes[:].bitcast(FP8X4), scales=scales[:], in_=grouped)
            return codes, scales

        def multiply(g, t):
            rows = slice(t * P, (t + 1) * P)
            nc.tensor.matmul_mx(
                out=acc[t][:],
                lhsT=y_codes[g][:, rows].bitcast(FP8X4),
                lhsT_scale=y_scales[g][:, rows],
                rhs=w_codes[g][:].bitcast(FP8X4),
                rhs_scale=w_scales[g][:],
                start=(g == 0),
                stop=(g == N_PASS - 1),
            )

        def in_range(g):
            return 0 <= g < N_PASS

        def closes_round(g):
            return in_range(g) and g % ROUND_PASSES == ROUND_PASSES - 1

        for r in range(LOAD_AHEAD):
            y_rows[r] = load_round(y_pool, y_lin, r)
            w_rows[r] = load_round(w_pool, W2, r)
        vectors = const.tile([P, PAIR * P], BF16)
        nc.scalar.dma_start(out=vectors[0 : P // 2, :], in_=gamma.rearrange("(r c) -> r c", c=PAIR * P))
        nc.scalar.dma_start(out=vectors[P // 2 : P, :], in_=beta.rearrange("(r c) -> r c", c=PAIR * P))
        identity = const.tile([P, P], F32)
        make_identity(nc, identity[:])
        one = const.tile([P, 1], F32)
        nc.vector.memset(one[:], 1.0)
        nc.scalar.activation(out=one[:], in_=one[:], func=ACT.Sqrt)
        bank = vector_banks.tile([P, BATCH], F32, tag="bank")
        nc.tensor.transpose(bank[:, 0:P], vectors[:].bitcast(F32), identity[:])
        gamma_beta = const.tile([P, PAIR * P], F32)
        nc.vector.tensor_copy(out=gamma_beta[:], in_=bank[:].bitcast(BF16)[:, 0 : PAIR * P])
        acc = [acc_pool.tile([P, WIDTH], F32, name="acc%d" % t) for t in range(ROW_TILES)]

        for i in range(-STATS_LEAD, N_PASS + MATMUL_LAG):
            g_stats = i + STATS_LEAD
            g_weight = i + WEIGHT_LEAD
            g_group = i - GROUP_LAG
            g_multiply = i - MATMUL_LAG
            for g, rows, pool, source in ((g_stats, y_rows, y_pool, y_lin), (g_weight, w_rows, w_pool, W2)):
                r = g // ROUND_PASSES + LOAD_AHEAD
                if in_range(g) and g % ROUND_PASSES == 0 and r < N_ROUNDS:
                    rows[r] = load_round(pool, source, r)

            if in_range(g_group):
                grouped = shared.tile([P, BATCH, PACK], BF16, tag="a_grouped", align_bytes=64)
                a_grouped[g_group] = grouped
                nc.gpsimd.tensor_scalar(
                    out=grouped[:, VECTOR_ROWS:BATCH, :],
                    in0=a_planes[g_group][:, :, VECTOR_ROWS:BATCH].rearrange("p t b -> p b t"),
                    scalar1=1.0,
                    scalar2=0.0,
                    op0=ALU.mult,
                    op1=ALU.add,
                )
            if closes_round(g_stats - 3):
                invert_deviation((g_stats - 3) // ROUND_PASSES)
                scale_and_shift((g_stats - 3) // ROUND_PASSES)

            for u in range(HALVES):
                if in_range(g_weight):
                    copy_weights(g_weight, u)
                if in_range(g_stats):
                    read_statistics(g_stats, u)
            if in_range(i):
                for u in range(HALVES):
                    normalise(i, u)
            if in_range(g_multiply):
                for t in range(ROW_TILES):
                    multiply(g_multiply, t)

            if closes_round(g_stats):
                merge_statistics(g_stats // ROUND_PASSES)
            if closes_round(g_stats - 1):
                root_of_variance((g_stats - 1) // ROUND_PASSES)

            if in_range(g_group):
                nc.vector.tensor_copy(
                    out=a_grouped[g_group][:, 0:VECTOR_ROWS, :].rearrange("p (c j) t -> p c t j", j=RUN),
                    in_=a_planes[g_group][:, :, 0:VECTOR_ROWS].rearrange("p t (c j) -> p c t j", j=RUN),
                )
            if in_range(g_weight - 1):
                w_codes[g_weight - 1], w_scales[g_weight - 1] = quantise(
                    w_mx, w_grouped[g_weight - 1][:], WIDTH, "w"
                )
            if in_range(g_group):
                y_codes[g_group], y_scales[g_group] = quantise(
                    y_mx, a_grouped[g_group][:].rearrange("p b t -> p (b t)"), BATCH, "y"
                )

        bias_rows = const.tile([P, WIDTH], BF16)
        nc.sync.dma_start(out=bias_rows[:], in_=b2.partition_broadcast(P))
        logits = []
        sum_squares = const.tile([P, ROW_TILES], F32)
        norm = const.tile([P, ROW_TILES], F32)
        factor = const.tile([P, ROW_TILES], F32)
        for t in range(ROW_TILES):
            p_rows = tail.tile([P, WIDTH], F32, tag="p_rows")
            nc.vector.tensor_tensor(out=p_rows[:], in0=acc[t][:], in1=bias_rows[:], op=ALU.add)
            squares = tail.tile([P, WIDTH], F32, tag="squares")
            nc.scalar.activation(
                out=squares[:], in_=p_rows[:], func=ACT.Square, accum_out=sum_squares[:, t : t + 1]
            )
            nc.scalar.activation(out=norm[:, t : t + 1], in_=sum_squares[:, t : t + 1], func=ACT.Sqrt)
            logits.append(p_rows)
        for t in range(ROW_TILES):
            nc.vector.tensor_scalar_max(out=factor[:, t : t + 1], in0=norm[:, t : t + 1], scalar1=L2_EPS)
            nc.vector.reciprocal(out=factor[:, t : t + 1], in_=factor[:, t : t + 1])
            nc.vector.tensor_scalar_mul(out=logits[t][:], in0=logits[t][:], scalar1=factor[:, t : t + 1])
            nc.sync.dma_start(out=out[t * P : (t + 1) * P, :], in_=logits[t][:])
